import numpy as np
import ml_dtypes


def mxq(x, axis, fmt="e4m3"):
    dtype, down = {"e4m3": (ml_dtypes.float8_e4m3fn, 7), "e5m2": (ml_dtypes.float8_e5m2, 14)}[fmt]
    v = np.moveaxis(np.asarray(x, np.float32).astype(ml_dtypes.bfloat16).astype(np.float64), axis, -1)
    blocks = v.reshape(v.shape[:-1] + (-1, 32))
    amax = np.abs(blocks).max(-1, keepdims=True)
    byte = np.maximum(np.where(amax > 0, np.frexp(amax)[1] - 1 + 127, 0) - down, 1)
    scale = np.exp2(byte - 127.0)
    codes = (blocks / scale).astype(np.float32).astype(dtype).astype(np.float64)
    return np.moveaxis((codes * scale).reshape(v.shape), -1, axis)


WIDE = False


def mx_kscale(k):
    if not WIDE:
        return np.ones(k)
    levels = np.array([10, -10, 5, -5, 0])
    a = np.random.permutation(np.resize(levels, k // 512 * 4)).reshape(k // 512, 4)
    idx = np.arange(k)
    return np.exp2(a[idx // 512, idx % 128 // 32])


BF16 = ml_dtypes.bfloat16


def bf(x):
    return np.asarray(x, np.float32).astype(BF16)


def f64(x):
    return np.asarray(x).astype(np.float64)


E2M1 = np.array([0.0, 0.5, 1.0, 1.5, 2.0, 3.0, 4.0, 6.0, -0.0, -0.5, -1.0, -1.5, -2.0, -3.0, -4.0, -6.0])


def pack_weight(w, fmt):
    k, n = w.shape
    w = f64(bf(w)).reshape(k // 32, 32, n)
    amax = np.abs(w).max(1)
    if fmt == "e4m3":
        byte = np.frexp(amax)[1] - 1 + 127 - 7
    else:
        mant, ex = np.frexp(amax / 6.0)
        byte = np.where(mant > 0.5, ex, ex - 1) + 127
    byte = np.clip(np.where(amax > 0, byte, 1), 1, 254)
    scaled = (w * np.exp2(127.0 - byte)[:, None, :]).reshape(k, n).astype(np.float32)
    by_word = np.ascontiguousarray(scaled.reshape(k // 512, 128, 4, n).transpose(0, 1, 3, 2))
    if fmt == "e4m3":
        words = by_word.astype(ml_dtypes.float8_e4m3fn).view(np.uint8)
    else:
        c = by_word.astype(ml_dtypes.float4_e2m1fn).view(np.uint8) & 0xF
        words = c[..., 0::2] | (c[..., 1::2] << 4)
    return np.ascontiguousarray(words), np.ascontiguousarray(byte.astype(np.uint8).reshape(k // 512, 16, n))


def unpack_weight(words, scales, fmt):
    g, p, n, _ = words.shape
    if fmt == "e4m3":
        vals = np.ascontiguousarray(words).view(ml_dtypes.float8_e4m3fn).astype(np.float64)
    else:
        nib = np.empty((g, p, n, 4), np.uint8)
        nib[..., 0::2] = words & 0xF
        nib[..., 1::2] = words >> 4
        vals = E2M1[nib]
    vals = vals * np.repeat(np.exp2(scales.astype(np.float64) - 127.0), 8, axis=1)[..., None]
    return vals.transpose(0, 1, 3, 2).reshape(g * 512, n)


B, IN, G, OUT = 128, 1024, 8, 2048
K = IN * G
GRID_MIN, GRID_MAX = -2.0, 2.0
H = (GRID_MAX - GRID_MIN) / (G - 1)


def setup_inputs():
    sf = mx_kscale(K)[::G]
    a = np.log2(sf.max() / sf)
    grid = bf(np.linspace(GRID_MIN, GRID_MAX, G) + 0.02 * np.random.standard_normal(G))
    z = np.random.standard_normal((B, IN))
    far = f64(grid).max() + H * np.sqrt(a * np.log(2.0)) + 0.05 * z
    x = np.where(a > 0, far, z)
    w = np.random.standard_normal((K, OUT)) / np.sqrt(IN) * np.repeat(np.exp2(a), G)[:, None]
    words, scales = pack_weight(w, "e4m3")
    return {"x": bf(x), "grid": grid, "spline_weight_words": words, "spline_weight_scales": scales}


def reference(x, grid, spline_weight_words, spline_weight_scales):
    h = (GRID_MAX - GRID_MIN) / (G - 1)
    basis = np.exp(-np.square((f64(x)[..., None] - f64(grid)) / h))
    return mxq(basis.reshape(basis.shape[0], -1), 1, "e4m3") @ unpack_weight(spline_weight_words, spline_weight_scales, "e4m3")

@@ -1,0 +1,155 @@
+from contextlib import ExitStack
+
+import concourse.mybir as mybir
+from concourse.masks import make_identity
+
+F32 = mybir.dt.float32
+BF16 = mybir.dt.bfloat16
+I32 = mybir.dt.int32
+U32 = mybir.dt.uint32
+U8 = mybir.dt.uint8
+FP8X4 = mybir.dt.float8_e4m3fn_x4
+ACT = mybir.ActivationFunctionType
+ALU = mybir.AluOpType
+
+P = 128
+B = 128
+IN = 1024
+GRID = 8
+OUT = 2048
+PACK = 4
+K_PASS = P * PACK
+PASSES = IN * GRID // K_PASS
+FEATURES = K_PASS // GRID
+N_TILE = 512
+N_TILES = OUT // N_TILE
+ROUND = 4
+ROUNDS = PASSES // ROUND
+QUADRANTS = 4
+INV_H = (GRID - 1) / 4.0
+WORDS_BEFORE_SCALES = 2
+
+FLOPS = 2 * B * IN * GRID * OUT
+
+
+def tile_gaussiankernel_w_kernel(
+    tc, x, grid, spline_weight_words, spline_weight_scales, out
+):
+    nc = tc.nc
+    with ExitStack() as ctx:
+        const = ctx.enter_context(tc.tile_pool(name="const", bufs=1))
+        weights = ctx.enter_context(tc.tile_pool(name="weights", bufs=PASSES))
+        work = ctx.enter_context(tc.tile_pool(name="work", bufs=2))
+        results = ctx.enter_context(tc.tile_pool(name="results", bufs=N_TILES))
+        xt_banks = ctx.enter_context(tc.psum_pool(name="xt_banks", bufs=ROUNDS))
+        acc_banks = ctx.enter_context(tc.psum_pool(name="acc_banks", bufs=N_TILES))
+        ctx.enter_context(tc.manual_schedule())
+
+        ident = const.tile([P, P], BF16)
+        make_identity(nc, ident[:])
+
+        w_planes = const.tile([P, ROUNDS, OUT], U8, align_bytes=64)
+        nc.vector.memset(w_planes[:].rearrange("p c n -> p (c n)").bitcast(I32), 0)
+
+        grid_col = const.tile([P, PACK], BF16)
+        for half in range(2):
+            nc.scalar.dma_start(
+                out=grid_col[half:P:2, :],
+                in_=grid[PACK * half : PACK * (half + 1)].partition_broadcast(P // 2),
+            )
+
+        x_sb = const.tile([P, IN], BF16)
+        nc.sync.dma_start(out=x_sb[:], in_=x)
+
+        words_i32 = spline_weight_words.rearrange("g p n t -> g p (n t)").bitcast(I32)
+        w_words = []
+        for g in range(PASSES):
+            if g == WORDS_BEFORE_SCALES:
+                for c in range(ROUNDS):
+                    for quadrant in range(QUADRANTS):
+                        nc.sync.dma_start(
+                            out=w_planes[32 * quadrant : 32 * quadrant + 16, c, :].bitcast(I32),
+                            in_=spline_weight_scales[
+                                ROUND * c : ROUND * (c + 1), 4 * quadrant : 4 * (quadrant + 1), :
+                            ].bitcast(I32),
+                        )
+            w = weights.tile([P, OUT * PACK], U8, name="w", align_bytes=64)
+            nc.sync.dma_start(out=w[:].bitcast(I32), in_=words_i32[g])
+            w_words.append(w)
+
+        x_twice = const.tile([P, IN, 2], BF16)
+        xt = []
+        for r in range(ROUNDS):
+            feats = slice(ROUND * FEATURES * r, ROUND * FEATURES * (r + 1))
+            nc.vector.tensor_copy(
+                out=x_twice[:, feats, :],
+                in_=x_sb[:, feats].unsqueeze(2).to_broadcast([P, ROUND * FEATURES, 2]),
+            )
+            bank = xt_banks.tile([P, ROUND * B], BF16, name="xt")
+            for o in range(ROUND):
+                g = ROUND * r + o
+                nc.tensor.transpose(
+                    out=bank[:, B * o : B * (o + 1)],
+                    in_=x_twice[:, FEATURES * g : FEATURES * (g + 1), :].rearrange(
+                        "b i two -> b (i two)"
+                    ),
+                    identity=ident[:],
+                )
+            xt.append(bank)
+
+        b_codes = const.tile([P, PASSES * B], U32, align_bytes=64)
+        b_scales = const.tile([P, PASSES * B], U8, align_bytes=64)
+        shape = [P, ROUND * B, PACK]
+
+        def distances(r):
+            u = work.tile(shape, F32, name="u")
+            nc.vector.tensor_tensor(
+                out=u[:],
+                in0=xt[r][:].unsqueeze(2).to_broadcast(shape),
+                in1=grid_col[:].unsqueeze(1).to_broadcast(shape),
+                op=ALU.subtract,
+            )
+            return u
+
+        def quantised_basis(r, u):
+            flat = u[:].rearrange("p c t -> p (c t)")
+            nc.scalar.activation(out=flat, in_=flat, func=ACT.Square, scale=INV_H)
+            basis = work.tile([P, ROUND * B * PACK], BF16, name="basis", align_bytes=64)
+            nc.scalar.activation(out=basis[:], in_=flat, func=ACT.Exp, scale=-1.0)
+            cols = slice(ROUND * B * r, ROUND * B * (r + 1))
+            nc.vector.quantize_mx(
+                out=b_codes[:, cols].bitcast(FP8X4), scales=b_scales[:, cols], in_=basis[:]
+            )
+
+        u_next = distances(0)
+        for r in range(ROUNDS):
+            u_now = u_next
+            if r + 1 < ROUNDS:
+                u_next = distances(r + 1)
+            quantised_basis(r, u_now)
+
+        acc = []
+        for n in range(N_TILES):
+            bank = acc_banks.tile([P, N_TILE], F32, name="acc")
+            acc.append(bank)
+        for g in range(PASSES):
+            c, o = divmod(g, ROUND)
+            rows_b = slice(B * g, B * (g + 1))
+            for n in range(N_TILES):
+                nc.tensor.matmul_mx(
+                    out=acc[n][:],
+                    lhsT=b_codes[:, rows_b].bitcast(FP8X4),
+                    lhsT_scale=b_scales[:, rows_b],
+                    rhs=w_words[g][:, PACK * N_TILE * n : PACK * N_TILE * (n + 1)].bitcast(FP8X4),
+                    rhs_scale=w_planes[4 * o : P, c, N_TILE * n : N_TILE * (n + 1)],
+                    start=(g == 0),
+                    stop=(g == PASSES - 1),
+                )
+
+        for n in range(N_TILES):
+            res = results.tile([P, N_TILE], F32, name="res")
+            if n % 2 == 0:
+                nc.vector.tensor_copy(out=res[:], in_=acc[n][:])
+            else:
+                nc.scalar.copy(out=res[:], in_=acc[n][:])
+            nc.sync.dma_start(out=out[:, N_TILE * n : N_TILE * (n + 1)], in_=res[:])

@@ -28,6 +28,9 @@ ROUNDS = PASSES // ROUND
 QUADRANTS = 4
 INV_H = (GRID - 1) / 4.0
 WORDS_BEFORE_SCALES = 2
+SPLIT = 12
+EARLY_TILES = N_TILES - 1
+LATE_GROUPS = ((12, 13), (14,), (15,))
 
 FLOPS = 2 * B * IN * GRID * OUT
 
@@ -38,7 +41,9 @@ def tile_gaussiankernel_w_kernel(
     nc = tc.nc
     with ExitStack() as ctx:
         const = ctx.enter_context(tc.tile_pool(name="const", bufs=1))
-        weights = ctx.enter_context(tc.tile_pool(name="weights", bufs=PASSES))
+        weights = ctx.enter_context(tc.tile_pool(name="weights", bufs=SPLIT))
+        most = ctx.enter_context(tc.tile_pool(name="most", bufs=PASSES - SPLIT))
+        late = ctx.enter_context(tc.tile_pool(name="late", bufs=len(LATE_GROUPS)))
         work = ctx.enter_context(tc.tile_pool(name="work", bufs=2))
         results = ctx.enter_context(tc.tile_pool(name="results", bufs=N_TILES))
         xt_banks = ctx.enter_context(tc.psum_pool(name="xt_banks", bufs=ROUNDS))
@@ -73,9 +78,28 @@ def tile_gaussiankernel_w_kernel(
                                 ROUND * c : ROUND * (c + 1), 4 * quadrant : 4 * (quadrant + 1), :
                             ].bitcast(I32),
                         )
-            w = weights.tile([P, OUT * PACK], U8, name="w", align_bytes=64)
-            nc.sync.dma_start(out=w[:].bitcast(I32), in_=words_i32[g])
+            if g < SPLIT:
+                w = weights.tile([P, OUT * PACK], U8, name="w", align_bytes=64)
+                nc.sync.dma_start(out=w[:].bitcast(I32), in_=words_i32[g])
+            else:
+                w = most.tile([P, EARLY_TILES * N_TILE * PACK], U8, name="w_most", align_bytes=64)
+                nc.sync.dma_start(
+                    out=w[:].bitcast(I32), in_=words_i32[g][:, 0 : EARLY_TILES * N_TILE]
+                )
             w_words.append(w)
+        w_late = {}
+        for group in LATE_GROUPS:
+            t = late.tile([P, len(group), N_TILE * PACK], U8, name="w_late", align_bytes=64)
+            nc.sync.dma_start(
+                out=t[:].rearrange("p g b -> p (g b)").bitcast(I32).rearrange(
+                    "p (g n) -> p g n", g=len(group)
+                ),
+                in_=words_i32[group[0] : group[-1] + 1, :, EARLY_TILES * N_TILE : OUT].rearrange(
+                    "g p n -> p g n"
+                ),
+            )
+            for i, g in enumerate(group):
+                w_late[g] = t[:, i, :]
 
         x_twice = const.tile([P, IN, 2], BF16)
         xt = []
@@ -132,24 +156,33 @@ def tile_gaussiankernel_w_kernel(
         for n in range(N_TILES):
             bank = acc_banks.tile([P, N_TILE], F32, name="acc")
             acc.append(bank)
-        for g in range(PASSES):
+
+        def multiply(g, n, words):
             c, o = divmod(g, ROUND)
             rows_b = slice(B * g, B * (g + 1))
-            for n in range(N_TILES):
-                nc.tensor.matmul_mx(
-                    out=acc[n][:],
-                    lhsT=b_codes[:, rows_b].bitcast(FP8X4),
-                    lhsT_scale=b_scales[:, rows_b],
-                    rhs=w_words[g][:, PACK * N_TILE * n : PACK * N_TILE * (n + 1)].bitcast(FP8X4),
-                    rhs_scale=w_planes[4 * o : P, c, N_TILE * n : N_TILE * (n + 1)],
-                    start=(g == 0),
-                    stop=(g == PASSES - 1),
-                )
+            nc.tensor.matmul_mx(
+                out=acc[n][:],
+                lhsT=b_codes[:, rows_b].bitcast(FP8X4),
+                lhsT_scale=b_scales[:, rows_b],
+                rhs=words.bitcast(FP8X4),
+                rhs_scale=w_planes[4 * o : P, c, N_TILE * n : N_TILE * (n + 1)],
+                start=(g == 0),
+                stop=(g == PASSES - 1),
+            )
 
-        for n in range(N_TILES):
+        def store(n):
             res = results.tile([P, N_TILE], F32, name="res")
             if n % 2 == 0:
                 nc.vector.tensor_copy(out=res[:], in_=acc[n][:])
             else:
                 nc.scalar.copy(out=res[:], in_=acc[n][:])
             nc.sync.dma_start(out=out[:, N_TILE * n : N_TILE * (n + 1)], in_=res[:])
+
+        for g in range(PASSES):
+            for n in range(N_TILES if g < SPLIT else EARLY_TILES):
+                multiply(g, n, w_words[g][:, PACK * N_TILE * n : PACK * N_TILE * (n + 1)])
+        for n in range(EARLY_TILES):
+            store(n)
+        for g in range(SPLIT, PASSES):
+            multiply(g, EARLY_TILES, w_late[g])
+        store(EARLY_TILES)

@@ -28,6 +28,7 @@ ROUNDS = PASSES // ROUND
 QUADRANTS = 4
 INV_H = (GRID - 1) / 4.0
 WORDS_BEFORE_SCALES = 2
+WHOLE_GROUPS = ((0,), (1,), (2, 3, 4, 5), (6, 7, 8, 9), (10, 11))
 SPLIT = 12
 EARLY_TILES = N_TILES - 1
 LATE_GROUPS = ((12, 13), (14,), (15,))
@@ -41,7 +42,7 @@ def tile_gaussiankernel_w_kernel(
     nc = tc.nc
     with ExitStack() as ctx:
         const = ctx.enter_context(tc.tile_pool(name="const", bufs=1))
-        weights = ctx.enter_context(tc.tile_pool(name="weights", bufs=SPLIT))
+        weights = ctx.enter_context(tc.tile_pool(name="weights", bufs=1))
         most = ctx.enter_context(tc.tile_pool(name="most", bufs=PASSES - SPLIT))
         late = ctx.enter_context(tc.tile_pool(name="late", bufs=len(LATE_GROUPS)))
         work = ctx.enter_context(tc.tile_pool(name="work", bufs=2))
@@ -68,8 +69,8 @@ def tile_gaussiankernel_w_kernel(
 
         words_i32 = spline_weight_words.rearrange("g p n t -> g p (n t)").bitcast(I32)
         w_words = []
-        for g in range(PASSES):
-            if g == WORDS_BEFORE_SCALES:
+        for group in WHOLE_GROUPS:
+            if group[0] == WORDS_BEFORE_SCALES:
                 for c in range(ROUNDS):
                     for quadrant in range(QUADRANTS):
                         nc.sync.dma_start(
@@ -78,15 +79,21 @@ def tile_gaussiankernel_w_kernel(
                                 ROUND * c : ROUND * (c + 1), 4 * quadrant : 4 * (quadrant + 1), :
                             ].bitcast(I32),
                         )
-            if g < SPLIT:
-                w = weights.tile([P, OUT * PACK], U8, name="w", align_bytes=64)
-                nc.sync.dma_start(out=w[:].bitcast(I32), in_=words_i32[g])
-            else:
-                w = most.tile([P, EARLY_TILES * N_TILE * PACK], U8, name="w_most", align_bytes=64)
-                nc.sync.dma_start(
-                    out=w[:].bitcast(I32), in_=words_i32[g][:, 0 : EARLY_TILES * N_TILE]
-                )
-            w_words.append(w)
+            w = weights.tile(
+                [P, len(group), OUT * PACK], U8, name="w%d" % group[0], align_bytes=64
+            )
+            nc.sync.dma_start(
+                out=w[:].rearrange("p g b -> p (g b)").bitcast(I32).rearrange(
+                    "p (g n) -> p g n", g=len(group)
+                ),
+                in_=words_i32[group[0] : group[-1] + 1].rearrange("g p n -> p g n"),
+            )
+            for i in range(len(group)):
+                w_words.append(w[:, i, :])
+        for g in range(SPLIT, PASSES):
+            w = most.tile([P, EARLY_TILES * N_TILE * PACK], U8, name="w_most", align_bytes=64)
+            nc.sync.dma_start(out=w[:].bitcast(I32), in_=words_i32[g][:, 0 : EARLY_TILES * N_TILE])
+            w_words.append(w[:])
         w_late = {}
         for group in LATE_GROUPS:
             t = late.tile([P, len(group), N_TILE * PACK], U8, name="w_late", align_bytes=64)

@@ -28,7 +28,7 @@ ROUNDS = PASSES // ROUND
 QUADRANTS = 4
 INV_H = (GRID - 1) / 4.0
 WORDS_BEFORE_SCALES = 2
-WHOLE_GROUPS = ((0,), (1,), (2, 3, 4, 5), (6, 7, 8, 9), (10, 11))
+WHOLE_GROUPS = ((0,), (1,), (2, 3), (4, 5), (6, 7), (8, 9), (10, 11))
 SPLIT = 12
 EARLY_TILES = N_TILES - 1
 LATE_GROUPS = ((12, 13), (14,), (15,))

@@ -27,7 +27,6 @@ ROUND = 4
 ROUNDS = PASSES // ROUND
 QUADRANTS = 4
 INV_H = (GRID - 1) / 4.0
-WORDS_BEFORE_SCALES = 2
 WHOLE_GROUPS = ((0,), (1,), (2, 3), (4, 5), (6, 7), (8, 9), (10, 11))
 SPLIT = 12
 EARLY_TILES = N_TILES - 1
@@ -56,6 +55,14 @@ def tile_gaussiankernel_w_kernel(
 
         w_planes = const.tile([P, ROUNDS, OUT], U8, align_bytes=64)
         nc.vector.memset(w_planes[:].rearrange("p c n -> p (c n)").bitcast(I32), 0)
+        for c in range(ROUNDS):
+            for quadrant in range(QUADRANTS):
+                nc.gpsimd.dma_start(
+                    out=w_planes[32 * quadrant : 32 * quadrant + 16, c, :].bitcast(F32),
+                    in_=spline_weight_scales[
+                        ROUND * c : ROUND * (c + 1), 4 * quadrant : 4 * (quadrant + 1), :
+                    ].bitcast(F32),
+                )
 
         grid_col = const.tile([P, PACK], BF16)
         for half in range(2):
@@ -70,15 +77,6 @@ def tile_gaussiankernel_w_kernel(
         words_i32 = spline_weight_words.rearrange("g p n t -> g p (n t)").bitcast(I32)
         w_words = []
         for group in WHOLE_GROUPS:
-            if group[0] == WORDS_BEFORE_SCALES:
-                for c in range(ROUNDS):
-                    for quadrant in range(QUADRANTS):
-                        nc.sync.dma_start(
-                            out=w_planes[32 * quadrant : 32 * quadrant + 16, c, :].bitcast(I32),
-                            in_=spline_weight_scales[
-                                ROUND * c : ROUND * (c + 1), 4 * quadrant : 4 * (quadrant + 1), :
-                            ].bitcast(I32),
-                        )
             w = weights.tile(
                 [P, len(group), OUT * PACK], U8, name="w%d" % group[0], align_bytes=64
             )

@@ -30,7 +30,10 @@ INV_H = (GRID - 1) / 4.0
 WHOLE_GROUPS = ((0,), (1,), (2, 3), (4, 5), (6, 7), (8, 9), (10, 11))
 SPLIT = 12
 EARLY_TILES = N_TILES - 1
-LATE_GROUPS = ((12, 13), (14,), (15,))
+EARLY = EARLY_TILES * N_TILE
+HALF = N_TILE // 2
+GROUPS = ((0, N_TILE), (N_TILE, N_TILE), (2 * N_TILE, N_TILE), (EARLY, HALF), (EARLY + HALF, HALF))
+LATE_LOADS = ((12, 2, EARLY, N_TILE), (14, 1, EARLY, N_TILE), (15, 1, EARLY, HALF), (15, 1, EARLY + HALF, HALF))
 
 FLOPS = 2 * B * IN * GRID * OUT
 
@@ -43,11 +46,11 @@ def tile_gaussiankernel_w_kernel(
         const = ctx.enter_context(tc.tile_pool(name="const", bufs=1))
         weights = ctx.enter_context(tc.tile_pool(name="weights", bufs=1))
         most = ctx.enter_context(tc.tile_pool(name="most", bufs=PASSES - SPLIT))
-        late = ctx.enter_context(tc.tile_pool(name="late", bufs=len(LATE_GROUPS)))
+        late = ctx.enter_context(tc.tile_pool(name="late", bufs=len(LATE_LOADS)))
         work = ctx.enter_context(tc.tile_pool(name="work", bufs=2))
-        results = ctx.enter_context(tc.tile_pool(name="results", bufs=N_TILES))
-        xt_banks = ctx.enter_context(tc.psum_pool(name="xt_banks", bufs=ROUNDS))
-        acc_banks = ctx.enter_context(tc.psum_pool(name="acc_banks", bufs=N_TILES))
+        results = ctx.enter_context(tc.tile_pool(name="results", bufs=len(GROUPS)))
+        xt_banks = ctx.enter_context(tc.psum_pool(name="xt_banks", bufs=8 - len(GROUPS)))
+        acc_banks = ctx.enter_context(tc.psum_pool(name="acc_banks", bufs=len(GROUPS)))
         ctx.enter_context(tc.manual_schedule())
 
         ident = const.tile([P, P], BF16)
@@ -93,18 +96,19 @@ def tile_gaussiankernel_w_kernel(
             nc.sync.dma_start(out=w[:].bitcast(I32), in_=words_i32[g][:, 0 : EARLY_TILES * N_TILE])
             w_words.append(w[:])
         w_late = {}
-        for group in LATE_GROUPS:
-            t = late.tile([P, len(group), N_TILE * PACK], U8, name="w_late", align_bytes=64)
+        for g0, passes, col0, cols in LATE_LOADS:
+            t = late.tile([P, passes, cols * PACK], U8, name="w_late", align_bytes=64)
             nc.sync.dma_start(
                 out=t[:].rearrange("p g b -> p (g b)").bitcast(I32).rearrange(
-                    "p (g n) -> p g n", g=len(group)
+                    "p (g n) -> p g n", g=passes
                 ),
-                in_=words_i32[group[0] : group[-1] + 1, :, EARLY_TILES * N_TILE : OUT].rearrange(
-                    "g p n -> p g n"
-                ),
+                in_=words_i32[g0 : g0 + passes, :, col0 : col0 + cols].rearrange("g p n -> p g n"),
             )
-            for i, g in enumerate(group):
-                w_late[g] = t[:, i, :]
+            for i in range(passes):
+                for first in range(col0, col0 + cols, HALF):
+                    w_late[(g0 + i, first)] = t[
+                        :, i, PACK * (first - col0) : PACK * (first - col0 + HALF)
+                    ]
 
         x_twice = const.tile([P, IN, 2], BF16)
         xt = []
@@ -158,36 +162,44 @@ def tile_gaussiankernel_w_kernel(
             quantised_basis(r, u_now)
 
         acc = []
-        for n in range(N_TILES):
-            bank = acc_banks.tile([P, N_TILE], F32, name="acc")
+        for first, width in GROUPS:
+            bank = acc_banks.tile([P, width], F32, name="acc")
             acc.append(bank)
 
         def multiply(g, n, words):
             c, o = divmod(g, ROUND)
+            first, width = GROUPS[n]
             rows_b = slice(B * g, B * (g + 1))
             nc.tensor.matmul_mx(
                 out=acc[n][:],
                 lhsT=b_codes[:, rows_b].bitcast(FP8X4),
                 lhsT_scale=b_scales[:, rows_b],
                 rhs=words.bitcast(FP8X4),
-                rhs_scale=w_planes[4 * o : P, c, N_TILE * n : N_TILE * (n + 1)],
+                rhs_scale=w_planes[4 * o : P, c, first : first + width],
                 start=(g == 0),
                 stop=(g == PASSES - 1),
             )
 
-        def store(n):
-            res = results.tile([P, N_TILE], F32, name="res")
-            if n % 2 == 0:
+        def store(n, engine):
+            first, width = GROUPS[n]
+            res = results.tile([P, width], F32, name="res")
+            if engine == "vector":
                 nc.vector.tensor_copy(out=res[:], in_=acc[n][:])
             else:
                 nc.scalar.copy(out=res[:], in_=acc[n][:])
-            nc.sync.dma_start(out=out[:, N_TILE * n : N_TILE * (n + 1)], in_=res[:])
+            nc.sync.dma_start(out=out[:, first : first + width], in_=res[:])
 
         for g in range(PASSES):
-            for n in range(N_TILES if g < SPLIT else EARLY_TILES):
-                multiply(g, n, w_words[g][:, PACK * N_TILE * n : PACK * N_TILE * (n + 1)])
-        for n in range(EARLY_TILES):
-            store(n)
-        for g in range(SPLIT, PASSES):
-            multiply(g, EARLY_TILES, w_late[g])
-        store(EARLY_TILES)
+            for n in range(len(GROUPS) if g < SPLIT else EARLY_TILES):
+                first, width = GROUPS[n]
+                multiply(g, n, w_words[g][:, PACK * first : PACK * (first + width)])
+        store(0, "vector")
+        store(1, "scalar")
+        store(2, "vector")
+        for g in range(SPLIT, PASSES - 1):
+            for n in (3, 4):
+                multiply(g, n, w_late[(g, GROUPS[n][0])])
+        multiply(PASSES - 1, 3, w_late[(PASSES - 1, GROUPS[3][0])])
+        store(3, "vector")
+        multiply(PASSES - 1, 4, w_late[(PASSES - 1, GROUPS[4][0])])
+        store(4, "scalar")

from contextlib import ExitStack

import concourse.mybir as mybir
from concourse.masks import make_identity

F32 = mybir.dt.float32
BF16 = mybir.dt.bfloat16
I32 = mybir.dt.int32
U32 = mybir.dt.uint32
U8 = mybir.dt.uint8
FP8X4 = mybir.dt.float8_e4m3fn_x4
ACT = mybir.ActivationFunctionType
ALU = mybir.AluOpType

P = 128
B = 128
IN = 1024
GRID = 8
OUT = 2048
PACK = 4
K_PASS = P * PACK
PASSES = IN * GRID // K_PASS
FEATURES = K_PASS // GRID
N_TILE = 512
N_TILES = OUT // N_TILE
ROUND = 4
ROUNDS = PASSES // ROUND
QUADRANTS = 4
INV_H = (GRID - 1) / 4.0
WHOLE_GROUPS = ((0,), (1,), (2, 3), (4, 5), (6, 7), (8, 9), (10, 11))
SPLIT = 12
EARLY_TILES = N_TILES - 1
EARLY = EARLY_TILES * N_TILE
HALF = N_TILE // 2
GROUPS = ((0, N_TILE), (N_TILE, N_TILE), (2 * N_TILE, N_TILE), (EARLY, HALF), (EARLY + HALF, HALF))
LATE_LOADS = ((12, 2, EARLY, N_TILE), (14, 1, EARLY, N_TILE), (15, 1, EARLY, HALF), (15, 1, EARLY + HALF, HALF))

FLOPS = 2 * B * IN * GRID * OUT


def tile_gaussiankernel_w_kernel(
    tc, x, grid, spline_weight_words, spline_weight_scales, out
):
    nc = tc.nc
    with ExitStack() as ctx:
        const = ctx.enter_context(tc.tile_pool(name="const", bufs=1))
        weights = ctx.enter_context(tc.tile_pool(name="weights", bufs=1))
        most = ctx.enter_context(tc.tile_pool(name="most", bufs=PASSES - SPLIT))
        late = ctx.enter_context(tc.tile_pool(name="late", bufs=len(LATE_LOADS)))
        work = ctx.enter_context(tc.tile_pool(name="work", bufs=2))
        results = ctx.enter_context(tc.tile_pool(name="results", bufs=len(GROUPS)))
        xt_banks = ctx.enter_context(tc.psum_pool(name="xt_banks", bufs=8 - len(GROUPS)))
        acc_banks = ctx.enter_context(tc.psum_pool(name="acc_banks", bufs=len(GROUPS)))
        ctx.enter_context(tc.manual_schedule())

        ident = const.tile([P, P], BF16)
        make_identity(nc, ident[:])

        w_planes = const.tile([P, ROUNDS, OUT], U8, align_bytes=64)
        nc.vector.memset(w_planes[:].rearrange("p c n -> p (c n)").bitcast(I32), 0)
        for c in range(ROUNDS):
            for quadrant in range(QUADRANTS):
                nc.gpsimd.dma_start(
                    out=w_planes[32 * quadrant : 32 * quadrant + 16, c, :].bitcast(F32),
                    in_=spline_weight_scales[
                        ROUND * c : ROUND * (c + 1), 4 * quadrant : 4 * (quadrant + 1), :
                    ].bitcast(F32),
                )

        grid_col = const.tile([P, PACK], BF16)
        for half in range(2):
            nc.scalar.dma_start(
                out=grid_col[half:P:2, :],
                in_=grid[PACK * half : PACK * (half + 1)].partition_broadcast(P // 2),
            )

        x_sb = const.tile([P, IN], BF16)
        nc.sync.dma_start(out=x_sb[:], in_=x)

        words_i32 = spline_weight_words.rearrange("g p n t -> g p (n t)").bitcast(I32)
        w_words = []
        for group in WHOLE_GROUPS:
            w = weights.tile(
                [P, len(group), OUT * PACK], U8, name="w%d" % group[0], align_bytes=64
            )
            nc.sync.dma_start(
                out=w[:].rearrange("p g b -> p (g b)").bitcast(I32).rearrange(
                    "p (g n) -> p g n", g=len(group)
                ),
                in_=words_i32[group[0] : group[-1] + 1].rearrange("g p n -> p g n"),
            )
            for i in range(len(group)):
                w_words.append(w[:, i, :])
        for g in range(SPLIT, PASSES):
            w = most.tile([P, EARLY_TILES * N_TILE * PACK], U8, name="w_most", align_bytes=64)
            nc.sync.dma_start(out=w[:].bitcast(I32), in_=words_i32[g][:, 0 : EARLY_TILES * N_TILE])
            w_words.append(w[:])
        w_late = {}
        for g0, passes, col0, cols in LATE_LOADS:
            t = late.tile([P, passes, cols * PACK], U8, name="w_late", align_bytes=64)
            nc.sync.dma_start(
                out=t[:].rearrange("p g b -> p (g b)").bitcast(I32).rearrange(
                    "p (g n) -> p g n", g=passes
                ),
                in_=words_i32[g0 : g0 + passes, :, col0 : col0 + cols].rearrange("g p n -> p g n"),
            )
            for i in range(passes):
                for first in range(col0, col0 + cols, HALF):
                    w_late[(g0 + i, first)] = t[
                        :, i, PACK * (first - col0) : PACK * (first - col0 + HALF)
                    ]

        x_twice = const.tile([P, IN, 2], BF16)
        xt = []
        for r in range(ROUNDS):
            feats = slice(ROUND * FEATURES * r, ROUND * FEATURES * (r + 1))
            nc.vector.tensor_copy(
                out=x_twice[:, feats, :],
                in_=x_sb[:, feats].unsqueeze(2).to_broadcast([P, ROUND * FEATURES, 2]),
            )
            bank = xt_banks.tile([P, ROUND * B], BF16, name="xt")
            for o in range(ROUND):
                g = ROUND * r + o
                nc.tensor.transpose(
                    out=bank[:, B * o : B * (o + 1)],
                    in_=x_twice[:, FEATURES * g : FEATURES * (g + 1), :].rearrange(
                        "b i two -> b (i two)"
                    ),
                    identity=ident[:],
                )
            xt.append(bank)

        b_codes = const.tile([P, PASSES * B], U32, align_bytes=64)
        b_scales = const.tile([P, PASSES * B], U8, align_bytes=64)
        shape = [P, ROUND * B, PACK]

        def distances(r):
            u = work.tile(shape, F32, name="u")
            nc.vector.tensor_tensor(
                out=u[:],
                in0=xt[r][:].unsqueeze(2).to_broadcast(shape),
                in1=grid_col[:].unsqueeze(1).to_broadcast(shape),
                op=ALU.subtract,
            )
            return u

        def quantised_basis(r, u):
            flat = u[:].rearrange("p c t -> p (c t)")
            nc.scalar.activation(out=flat, in_=flat, func=ACT.Square, scale=INV_H)
            basis = work.tile([P, ROUND * B * PACK], BF16, name="basis", align_bytes=64)
            nc.scalar.activation(out=basis[:], in_=flat, func=ACT.Exp, scale=-1.0)
            cols = slice(ROUND * B * r, ROUND * B * (r + 1))
            nc.vector.quantize_mx(
                out=b_codes[:, cols].bitcast(FP8X4), scales=b_scales[:, cols], in_=basis[:]
            )

        u_next = distances(0)
        for r in range(ROUNDS):
            u_now = u_next
            if r + 1 < ROUNDS:
                u_next = distances(r + 1)
            quantised_basis(r, u_now)

        acc = []
        for first, width in GROUPS:
            bank = acc_banks.tile([P, width], F32, name="acc")
            acc.append(bank)

        def multiply(g, n, words):
            c, o = divmod(g, ROUND)
            first, width = GROUPS[n]
            rows_b = slice(B * g, B * (g + 1))
            nc.tensor.matmul_mx(
                out=acc[n][:],
                lhsT=b_codes[:, rows_b].bitcast(FP8X4),
                lhsT_scale=b_scales[:, rows_b],
                rhs=words.bitcast(FP8X4),
                rhs_scale=w_planes[4 * o : P, c, first : first + width],
                start=(g == 0),
                stop=(g == PASSES - 1),
            )

        def store(n, engine):
            first, width = GROUPS[n]
            res = results.tile([P, width], F32, name="res")
            if engine == "vector":
                nc.vector.tensor_copy(out=res[:], in_=acc[n][:])
            else:
                nc.scalar.copy(out=res[:], in_=acc[n][:])
            nc.sync.dma_start(out=out[:, first : first + width], in_=res[:])

        for g in range(PASSES):
            for n in range(len(GROUPS) if g < SPLIT else EARLY_TILES):
                first, width = GROUPS[n]
                multiply(g, n, w_words[g][:, PACK * first : PACK * (first + width)])
        store(0, "vector")
        store(1, "scalar")
        store(2, "vector")
        for g in range(SPLIT, PASSES - 1):
            for n in (3, 4):
                multiply(g, n, w_late[(g, GROUPS[n][0])])
        multiply(PASSES - 1, 3, w_late[(PASSES - 1, GROUPS[3][0])])
        store(3, "vector")
        multiply(PASSES - 1, 4, w_late[(PASSES - 1, GROUPS[4][0])])
        store(4, "scalar")
